import numpy as np
import ml_dtypes


def mxq(x, axis, fmt="e4m3"):
    dtype, down = {"e4m3": (ml_dtypes.float8_e4m3fn, 7), "e5m2": (ml_dtypes.float8_e5m2, 14)}[fmt]
    v = np.moveaxis(np.asarray(x, np.float32).astype(ml_dtypes.bfloat16).astype(np.float64), axis, -1)
    blocks = v.reshape(v.shape[:-1] + (-1, 32))
    amax = np.abs(blocks).max(-1, keepdims=True)
    byte = np.maximum(np.where(amax > 0, np.frexp(amax)[1] - 1 + 127, 0) - down, 1)
    scale = np.exp2(byte - 127.0)
    codes = (blocks / scale).astype(np.float32).astype(dtype).astype(np.float64)
    return np.moveaxis((codes * scale).reshape(v.shape), -1, axis)


WIDE = False


def mx_kscale(k):
    if not WIDE:
        return np.ones(k)
    levels = np.array([10, -10, 5, -5, 0])
    if k % 512:
        return np.exp2(np.random.permutation(np.resize(levels, k // 32))).repeat(32)
    a = np.empty((k // 512, 16))
    for p in range(k // 512):
        a[p, :8] = np.random.permutation(np.resize(levels, 8))
        for g in range(8):
            far = levels[np.abs(levels - a[p, g]) >= 10]
            a[p, g + 8] = far[np.random.randint(len(far))]
    return np.exp2(a.ravel()).repeat(32)


BF16 = ml_dtypes.bfloat16


def bf(x):
    return np.asarray(x, np.float32).astype(BF16)


def f64(x):
    return np.asarray(x).astype(np.float64)


B, S, D, H, HD, M, G = 4, 128, 1024, 8, 128, 4096, 3
EPS = 1e-6


def rmsnorm(x, gain):
    var = np.mean(np.square(x), axis=-1, keepdims=True)
    return x * (1.0 / np.sqrt(var + EPS)) * gain


def setup_inputs():
    s = mx_kscale(D)
    return {"x": bf(np.random.standard_normal((B, S, D))),
            "rms1_scale": bf((1.0 + 0.1 * np.random.standard_normal(D)) * s),
            "w_qkv": bf(np.random.standard_normal((D, G * H * HD)) / np.sqrt(D) / s[:, None])}


def reference(x, rms1_scale, w_qkv):
    h = rmsnorm(f64(x), f64(rms1_scale))
    qkv = mxq(h, 2, "e4m3") @ mxq(f64(w_qkv), 0, "e4m3")
    qkv = qkv.reshape(B, S, G, H, HD)
    return qkv[:, :, 0], qkv[:, :, 1], qkv[:, :, 2]

@@ -1,0 +1,189 @@
+from contextlib import ExitStack
+
+import concourse.masks as masks
+import concourse.mybir as mybir
+
+BF16 = mybir.dt.bfloat16
+F32 = mybir.dt.float32
+U32 = mybir.dt.uint32
+U8 = mybir.dt.uint8
+I32 = mybir.dt.int32
+FP8X4 = mybir.dt.float8_e4m3fn_x4
+ACT = mybir.ActivationFunctionType
+ALU = mybir.AluOpType
+
+P = 128
+PACK = 4
+K_PASS = P * PACK
+BATCH = 4
+D = 1024
+PASSES = D // K_PASS
+PROJ = 3
+PROJ_COLS = 1024
+N_TILE = 512
+HALVES = PROJ_COLS // N_TILE
+RUN = 4
+SCALAR_COLS = 96
+VECTOR_RUNS = (N_TILE - SCALAR_COLS) // RUN
+UNITS = PROJ * HALVES
+SHARED_UNITS = 2
+EPS = 1e-6
+
+FLOPS = 2 * BATCH * P * D * PROJ * PROJ_COLS
+
+
+def tile_transformerblocktpu_pa_kernel(tc, x, rms1_scale, w_qkv, out_0, out_1, out_2):
+    nc = tc.nc
+    outs = [o.rearrange("b s h d -> b s (h d)") for o in (out_0, out_1, out_2)]
+    w_rows = w_qkv.rearrange("(c p t) n -> c p t n", t=PACK, p=P)
+
+    with ExitStack() as ctx:
+        const = ctx.enter_context(tc.tile_pool(name="const", bufs=1))
+        keep = ctx.enter_context(tc.tile_pool(name="keep", bufs=1))
+        per_batch = ctx.enter_context(tc.tile_pool(name="per_batch", bufs=BATCH))
+        w_in = ctx.enter_context(tc.tile_pool(name="w_in", bufs=PROJ * PASSES))
+        w_stage = ctx.enter_context(tc.tile_pool(name="w_stage", bufs=2 * PASSES))
+        out_stage = ctx.enter_context(tc.tile_pool(name="out_stage", bufs=2 * BATCH))
+        psum = ctx.enter_context(tc.psum_pool(name="psum", bufs=8))
+
+        gain_rows = const.tile([P, D], BF16)
+        nc.vector.memset(gain_rows[:].bitcast(I32), 0)
+        nc.sync.dma_start(out=gain_rows[0:1, :], in_=rms1_scale.rearrange("(o k) -> o k", o=1))
+        ones = const.tile([P, P], BF16)
+        nc.vector.memset(ones[:], 1.0)
+        eps = const.tile([P, 1], F32)
+        nc.vector.memset(eps[:], EPS)
+        identity = const.tile([P, P], F32)
+        masks.make_identity(nc, identity[:])
+        warm = const.tile([P, 1], F32)
+        nc.scalar.activation(out=warm[:], in_=eps[:], func=ACT.Sqrt)
+
+        x_sb = []
+        for b in range(BATCH):
+            x_tile = per_batch.tile([P, D], BF16, name="x_tile")
+            nc.sync.dma_start(out=x_tile[:], in_=x[b])
+            x_sb.append(x_tile)
+        w_raw = {}
+        for j in range(PROJ):
+            for c in range(PASSES):
+                raw = w_in.tile([P, PACK, PROJ_COLS], BF16, name="w_raw")
+                nc.sync.dma_start(
+                    out=raw[:], in_=w_rows[c, :, :, j * PROJ_COLS : (j + 1) * PROJ_COLS]
+                )
+                w_raw[(j, c)] = raw
+
+        gain_all = []
+        for bank in range(D // N_TILE):
+            spread = psum.tile([P, N_TILE], F32, tag="bank", name="spread")
+            nc.tensor.matmul(
+                out=spread[:],
+                lhsT=ones[:],
+                rhs=gain_rows[:, bank * N_TILE : (bank + 1) * N_TILE],
+                start=True,
+                stop=True,
+            )
+            gain_all.append(spread)
+
+        h_sb = []
+        for b in range(BATCH):
+            squares = per_batch.tile([P, D], BF16, name="squares")
+            mean_sq = per_batch.tile([P, 1], F32, name="mean_sq")
+            nc.scalar.activation(
+                out=squares[:],
+                in_=x_sb[b][:],
+                func=ACT.Square,
+                scale=D**-0.5,
+                accum_out=mean_sq[:],
+            )
+            rms = per_batch.tile([P, 1], F32, name="rms")
+            nc.scalar.activation(out=rms[:], in_=mean_sq[:], func=ACT.Sqrt, bias=eps[:])
+            inv_rms = per_batch.tile([P, 1], F32, name="inv_rms")
+            nc.vector.reciprocal(out=inv_rms[:], in_=rms[:])
+            h = per_batch.tile([P, D], BF16, name="h")
+            for bank in range(D // N_TILE):
+                feats = slice(bank * N_TILE, (bank + 1) * N_TILE)
+                nc.vector.scalar_tensor_tensor(
+                    out=h[:, feats],
+                    in0=x_sb[b][:, feats],
+                    scalar=inv_rms[:],
+                    in1=gain_all[bank][:],
+                    op0=ALU.mult,
+                    op1=ALU.mult,
+                )
+            h_sb.append(h)
+
+        h_grouped = keep.tile([P, BATCH, PASSES, P, PACK], BF16, align_bytes=64)
+        h_codes = keep.tile([P, BATCH, PASSES * P], U32, align_bytes=64)
+        h_scales = keep.tile([P, BATCH, PASSES * P], U8, align_bytes=64)
+        for b in range(BATCH):
+            words = h_sb[b][:].bitcast(F32)
+            h_t = psum.tile([P, PASSES, 2, P], F32, tag="bank", name="h_t")
+            for c in range(PASSES):
+                for u in range(2):
+                    w0 = c * (K_PASS // 2)
+                    nc.tensor.transpose(
+                        out=h_t[:, c, u, :],
+                        in_=words[:, w0 + u : w0 + K_PASS // 2 : 2],
+                        identity=identity[:],
+                    )
+            nc.scalar.copy(
+                out=h_grouped[:, b].rearrange("p c s t -> p (c s t)").bitcast(F32).rearrange(
+                    "p (c s u) -> p c s u", c=PASSES, u=2
+                ),
+                in_=h_t[:].rearrange("p c u s -> p c s u"),
+            )
+            nc.vector.quantize_mx(
+                out=h_codes[:, b, :].bitcast(FP8X4),
+                scales=h_scales[:, b, :],
+                in_=h_grouped[:, b].rearrange("p c s t -> p (c s t)"),
+            )
+
+        w_codes = keep.tile([P, UNITS, PASSES, N_TILE], U32, align_bytes=64)
+        w_scales = keep.tile([P, UNITS, PASSES, N_TILE], U8, align_bytes=64)
+
+        def prepare(u):
+            j, half = divmod(u, HALVES)
+            cols = slice(half * N_TILE, (half + 1) * N_TILE)
+            w_grouped = []
+            for c in range(PASSES):
+                grouped = w_stage.tile([P, N_TILE, PACK], BF16, align_bytes=64, name="grouped")
+                by_column = grouped[:].rearrange("p (a i) t -> p a t i", i=RUN)
+                by_row = w_raw[(j, c)][:, :, cols].rearrange("p t (a i) -> p a t i", i=RUN)
+                nc.vector.tensor_copy(out=by_column[:, :VECTOR_RUNS], in_=by_row[:, :VECTOR_RUNS])
+                nc.scalar.copy(out=by_column[:, VECTOR_RUNS:], in_=by_row[:, VECTOR_RUNS:])
+                w_grouped.append(grouped)
+            for c in range(PASSES):
+                nc.vector.quantize_mx(
+                    out=w_codes[:, u, c, :].bitcast(FP8X4),
+                    scales=w_scales[:, u, c, :],
+                    in_=w_grouped[c][:].rearrange("p n t -> p (n t)"),
+                )
+
+        def project(u):
+            j, half = divmod(u, HALVES)
+            cols = slice(half * N_TILE, (half + 1) * N_TILE)
+            accs = [psum.tile([P, N_TILE], F32, tag="bank", name="acc") for b in range(BATCH)]
+            for c in range(PASSES):
+                for b in range(BATCH):
+                    nc.tensor.matmul_mx(
+                        out=accs[b][:],
+                        lhsT=h_codes[:, b, c * P : (c + 1) * P].bitcast(FP8X4),
+                        lhsT_scale=h_scales[:, b, c * P : (c + 1) * P],
+                        rhs=w_codes[:, u, c, :].bitcast(FP8X4),
+                        rhs_scale=w_scales[:, u, c, :],
+                        start=(c == 0),
+                        stop=(c == PASSES - 1),
+                    )
+            for b in range(BATCH):
+                result = out_stage.tile([P, N_TILE], F32, name="result")
+                if u >= UNITS - SHARED_UNITS and b % 2 == 1:
+                    nc.vector.tensor_copy(out=result[:], in_=accs[b][:])
+                else:
+                    nc.scalar.copy(out=result[:], in_=accs[b][:])
+                nc.sync.dma_start(out=outs[j][b, :, cols], in_=result[:])
+
+        prepare(0)
+        for u in range(UNITS):
+            if u + 1 < UNITS:
+                prepare(u + 1)
+            project(u)

@@ -18,15 +18,16 @@ K_PASS = P * PACK
 BATCH = 4
 D = 1024
 PASSES = D // K_PASS
+GAIN_ROWS = D // P
 PROJ = 3
 PROJ_COLS = 1024
 N_TILE = 512
 HALVES = PROJ_COLS // N_TILE
 RUN = 4
-SCALAR_COLS = 96
-VECTOR_RUNS = (N_TILE - SCALAR_COLS) // RUN
+SCALAR_COLS = 112
 UNITS = PROJ * HALVES
 SHARED_UNITS = 2
+VECTOR_SQUARE = 1
 EPS = 1e-6
 
 FLOPS = 2 * BATCH * P * D * PROJ * PROJ_COLS
@@ -43,16 +44,16 @@ def tile_transformerblocktpu_pa_kernel(tc, x, rms1_scale, w_qkv, out_0, out_1, o
         per_batch = ctx.enter_context(tc.tile_pool(name="per_batch", bufs=BATCH))
         w_in = ctx.enter_context(tc.tile_pool(name="w_in", bufs=PROJ * PASSES))
         w_stage = ctx.enter_context(tc.tile_pool(name="w_stage", bufs=2 * PASSES))
-        out_stage = ctx.enter_context(tc.tile_pool(name="out_stage", bufs=2 * BATCH))
+        out_stage = ctx.enter_context(tc.tile_pool(name="out_stage", bufs=3 * BATCH))
         psum = ctx.enter_context(tc.psum_pool(name="psum", bufs=8))
+        ctx.enter_context(tc.manual_schedule())
 
-        gain_rows = const.tile([P, D], BF16)
+        gain_rows = const.tile([P, P], BF16)
         nc.vector.memset(gain_rows[:].bitcast(I32), 0)
-        nc.sync.dma_start(out=gain_rows[0:1, :], in_=rms1_scale.rearrange("(o k) -> o k", o=1))
-        ones = const.tile([P, P], BF16)
-        nc.vector.memset(ones[:], 1.0)
         eps = const.tile([P, 1], F32)
         nc.vector.memset(eps[:], EPS)
+        identity_bf16 = const.tile([P, P], BF16)
+        masks.make_identity(nc, identity_bf16[:])
         identity = const.tile([P, P], F32)
         masks.make_identity(nc, identity[:])
         warm = const.tile([P, 1], F32)
@@ -63,6 +64,10 @@ def tile_transformerblocktpu_pa_kernel(tc, x, rms1_scale, w_qkv, out_0, out_1, o
             x_tile = per_batch.tile([P, D], BF16, name="x_tile")
             nc.sync.dma_start(out=x_tile[:], in_=x[b])
             x_sb.append(x_tile)
+            if b == 0:
+                nc.sync.dma_start(
+                    out=gain_rows[0:GAIN_ROWS, :], in_=rms1_scale.rearrange("(r k) -> r k", k=P)
+                )
         w_raw = {}
         for j in range(PROJ):
             for c in range(PASSES):
@@ -75,47 +80,64 @@ def tile_transformerblocktpu_pa_kernel(tc, x, rms1_scale, w_qkv, out_0, out_1, o
         gain_all = []
         for bank in range(D // N_TILE):
             spread = psum.tile([P, N_TILE], F32, tag="bank", name="spread")
-            nc.tensor.matmul(
-                out=spread[:],
-                lhsT=ones[:],
-                rhs=gain_rows[:, bank * N_TILE : (bank + 1) * N_TILE],
-                start=True,
-                stop=True,
-            )
+            for i in range(N_TILE // P):
+                r = bank * (N_TILE // P) + i
+                nc.tensor.matmul(
+                    out=spread[:, i * P : (i + 1) * P],
+                    lhsT=identity_bf16[:, r : r + 1].to_broadcast([P, P]),
+                    rhs=gain_rows[:],
+                    start=True,
+                    stop=True,
+                )
             gain_all.append(spread)
 
-        h_sb = []
-        for b in range(BATCH):
+        mean_sq = [per_batch.tile([P, 1], F32, name="mean_sq") for b in range(BATCH)]
+        rms = [per_batch.tile([P, 1], F32, name="rms") for b in range(BATCH)]
+        h_sb = [per_batch.tile([P, D], BF16, name="h") for b in range(BATCH)]
+
+        def sum_squares(b):
             squares = per_batch.tile([P, D], BF16, name="squares")
-            mean_sq = per_batch.tile([P, 1], F32, name="mean_sq")
-            nc.scalar.activation(
-                out=squares[:],
-                in_=x_sb[b][:],
-                func=ACT.Square,
-                scale=D**-0.5,
-                accum_out=mean_sq[:],
-            )
-            rms = per_batch.tile([P, 1], F32, name="rms")
-            nc.scalar.activation(out=rms[:], in_=mean_sq[:], func=ACT.Sqrt, bias=eps[:])
+            if b == VECTOR_SQUARE:
+                nc.vector.scalar_tensor_tensor(
+                    out=squares[:],
+                    in0=x_sb[b][:],
+                    scalar=1.0 / D,
+                    in1=x_sb[b][:],
+                    op0=ALU.mult,
+                    op1=ALU.mult,
+                    accum_out=mean_sq[b][:],
+                )
+            else:
+                nc.scalar.activation(
+                    out=squares[:],
+                    in_=x_sb[b][:],
+                    func=ACT.Square,
+                    scale=D**-0.5,
+                    accum_out=mean_sq[b][:],
+                )
+
+        def root(b):
+            nc.scalar.activation(out=rms[b][:], in_=mean_sq[b][:], func=ACT.Sqrt, bias=eps[:])
+
+        def normalise(b):
             inv_rms = per_batch.tile([P, 1], F32, name="inv_rms")
-            nc.vector.reciprocal(out=inv_rms[:], in_=rms[:])
-            h = per_batch.tile([P, D], BF16, name="h")
+            nc.vector.reciprocal(out=inv_rms[:], in_=rms[b][:])
             for bank in range(D // N_TILE):
                 feats = slice(bank * N_TILE, (bank + 1) * N_TILE)
                 nc.vector.scalar_tensor_tensor(
-                    out=h[:, feats],
+                    out=h_sb[b][:, feats],
                     in0=x_sb[b][:, feats],
                     scalar=inv_rms[:],
                     in1=gain_all[bank][:],
                     op0=ALU.mult,
                     op1=ALU.mult,
                 )
-            h_sb.append(h)
 
         h_grouped = keep.tile([P, BATCH, PASSES, P, PACK], BF16, align_bytes=64)
         h_codes = keep.tile([P, BATCH, PASSES * P], U32, align_bytes=64)
         h_scales = keep.tile([P, BATCH, PASSES * P], U8, align_bytes=64)
-        for b in range(BATCH):
+
+        def turn(b):
             words = h_sb[b][:].bitcast(F32)
             h_t = psum.tile([P, PASSES, 2, P], F32, tag="bank", name="h_t")
             for c in range(PASSES):
@@ -126,12 +148,17 @@ def tile_transformerblocktpu_pa_kernel(tc, x, rms1_scale, w_qkv, out_0, out_1, o
                         in_=words[:, w0 + u : w0 + K_PASS // 2 : 2],
                         identity=identity[:],
                     )
+            return h_t
+
+        def collect(b, h_t):
             nc.scalar.copy(
                 out=h_grouped[:, b].rearrange("p c s t -> p (c s t)").bitcast(F32).rearrange(
                     "p (c s u) -> p c s u", c=PASSES, u=2
                 ),
                 in_=h_t[:].rearrange("p c u s -> p c s u"),
             )
+
+        def quantise_h(b):
             nc.vector.quantize_mx(
                 out=h_codes[:, b, :].bitcast(FP8X4),
                 scales=h_scales[:, b, :],
@@ -140,33 +167,48 @@ def tile_transformerblocktpu_pa_kernel(tc, x, rms1_scale, w_qkv, out_0, out_1, o
 
         w_codes = keep.tile([P, UNITS, PASSES, N_TILE], U32, align_bytes=64)
         w_scales = keep.tile([P, UNITS, PASSES, N_TILE], U8, align_bytes=64)
+        w_grouped = {}
+
+        def regroup(u, c, engine_copy, first, last):
+            j, half = divmod(u, HALVES)
+            if (u, c) not in w_grouped:
+                grouped = w_stage.tile([P, N_TILE, PACK], BF16, align_bytes=64, name="grouped")
+                w_grouped[(u, c)] = grouped
+            lo = half * N_TILE + first
+            hi = half * N_TILE + last
+            engine_copy(
+                w_grouped[(u, c)][:, first:last, :].rearrange("p (a i) t -> p a t i", i=RUN),
+                w_raw[(j, c)][:, :, lo:hi].rearrange("p t (a i) -> p a t i", i=RUN),
+            )
+
+        def gpsimd_copy(out, in_):
+            nc.gpsimd.tensor_scalar(
+                out=out, in0=in_, scalar1=1.0, scalar2=0.0, op0=ALU.mult, op1=ALU.add
+            )
+
+        def quantise_w(u, c):
+            nc.vector.quantize_mx(
+                out=w_codes[:, u, c, :].bitcast(FP8X4),
+                scales=w_scales[:, u, c, :],
+                in_=w_grouped[(u, c)][:].rearrange("p n t -> p (n t)"),
+            )
 
         def prepare(u):
-            j, half = divmod(u, HALVES)
-            cols = slice(half * N_TILE, (half + 1) * N_TILE)
-            w_grouped = []
+            s = 224 if u == 1 else SCALAR_COLS
             for c in range(PASSES):
-                grouped = w_stage.tile([P, N_TILE, PACK], BF16, align_bytes=64, name="grouped")
-                by_column = grouped[:].rearrange("p (a i) t -> p a t i", i=RUN)
-                by_row = w_raw[(j, c)][:, :, cols].rearrange("p t (a i) -> p a t i", i=RUN)
-                nc.vector.tensor_copy(out=by_column[:, :VECTOR_RUNS], in_=by_row[:, :VECTOR_RUNS])
-                nc.scalar.copy(out=by_column[:, VECTOR_RUNS:], in_=by_row[:, VECTOR_RUNS:])
-                w_grouped.append(grouped)
+                regroup(u, c, nc.vector.tensor_copy, 0, N_TILE - s)
+                regroup(u, c, nc.scalar.copy, N_TILE - s, N_TILE)
             for c in range(PASSES):
-                nc.vector.quantize_mx(
-                    out=w_codes[:, u, c, :].bitcast(FP8X4),
-                    scales=w_scales[:, u, c, :],
-                    in_=w_grouped[c][:].rearrange("p n t -> p (n t)"),
-                )
+                quantise_w(u, c)
 
         def project(u):
             j, half = divmod(u, HALVES)
             cols = slice(half * N_TILE, (half + 1) * N_TILE)
-            accs = [psum.tile([P, N_TILE], F32, tag="bank", name="acc") for b in range(BATCH)]
-            for c in range(PASSES):
-                for b in range(BATCH):
+            for b in range(BATCH):
+                acc = psum.tile([P, N_TILE], F32, tag="bank", name="acc")
+                for c in range(PASSES):
                     nc.tensor.matmul_mx(
-                        out=accs[b][:],
+                        out=acc[:],
                         lhsT=h_codes[:, b, c * P : (c + 1) * P].bitcast(FP8X4),
                         lhsT_scale=h_scales[:, b, c * P : (c + 1) * P],
                         rhs=w_codes[:, u, c, :].bitcast(FP8X4),
@@ -174,15 +216,42 @@ def tile_transformerblocktpu_pa_kernel(tc, x, rms1_scale, w_qkv, out_0, out_1, o
                         start=(c == 0),
                         stop=(c == PASSES - 1),
                     )
-            for b in range(BATCH):
                 result = out_stage.tile([P, N_TILE], F32, name="result")
                 if u >= UNITS - SHARED_UNITS and b % 2 == 1:
-                    nc.vector.tensor_copy(out=result[:], in_=accs[b][:])
+                    nc.vector.tensor_copy(out=result[:], in_=acc[:])
                 else:
-                    nc.scalar.copy(out=result[:], in_=accs[b][:])
+                    nc.scalar.copy(out=result[:], in_=acc[:])
                 nc.sync.dma_start(out=outs[j][b, :, cols], in_=result[:])
 
-        prepare(0)
+        sum_squares(0)
+        root(0)
+        sum_squares(VECTOR_SQUARE)
+        normalise(0)
+        turned = [turn(0)]
+        sum_squares(2)
+        root(1)
+        root(2)
+        normalise(1)
+        turned.append(turn(1))
+        sum_squares(3)
+        root(3)
+        normalise(2)
+        turned.append(turn(2))
+        normalise(3)
+        turned.append(turn(3))
+        regroup(0, 0, gpsimd_copy, 0, 512)
+        collect(0, turned[0])
+        collect(1, turned[1])
+        regroup(0, 1, nc.scalar.copy, 0, 192)
+        collect(2, turned[2])
+        collect(3, turned[3])
+        quantise_h(0)
+        quantise_h(1)
+        regroup(0, 1, nc.vector.tensor_copy, 192, N_TILE)
+        quantise_h(2)
+        quantise_w(0, 0)
+        quantise_h(3)
+        quantise_w(0, 1)
         for u in range(UNITS):
             if u + 1 < UNITS:
                 prepare(u + 1)

@@ -23,7 +23,7 @@ PROJ = 3
 PROJ_COLS = 1024
 N_TILE = 512
 HALVES = PROJ_COLS // N_TILE
-RUN = 4
+RUN = 8
 SCALAR_COLS = 112
 UNITS = PROJ * HALVES
 SHARED_UNITS = 2

@@ -26,7 +26,7 @@ HALVES = PROJ_COLS // N_TILE
 RUN = 8
 SCALAR_COLS = 112
 UNITS = PROJ * HALVES
-SHARED_UNITS = 2
+SHARED_UNITS = 1
 VECTOR_SQUARE = 1
 EPS = 1e-6
 
@@ -57,7 +57,7 @@ def tile_transformerblocktpu_pa_kernel(tc, x, rms1_scale, w_qkv, out_0, out_1, o
         identity = const.tile([P, P], F32)
         masks.make_identity(nc, identity[:])
         warm = const.tile([P, 1], F32)
-        nc.scalar.activation(out=warm[:], in_=eps[:], func=ACT.Sqrt)
+        nc.scalar.activation(out=warm[:], in_=eps[:], func=ACT.Abs_reciprocal_sqrt)
 
         x_sb = []
         for b in range(BATCH):
@@ -92,7 +92,7 @@ def tile_transformerblocktpu_pa_kernel(tc, x, rms1_scale, w_qkv, out_0, out_1, o
             gain_all.append(spread)
 
         mean_sq = [per_batch.tile([P, 1], F32, name="mean_sq") for b in range(BATCH)]
-        rms = [per_batch.tile([P, 1], F32, name="rms") for b in range(BATCH)]
+        inv_rms = [per_batch.tile([P, 1], F32, name="inv_rms") for b in range(BATCH)]
         h_sb = [per_batch.tile([P, D], BF16, name="h") for b in range(BATCH)]
 
         def sum_squares(b):
@@ -116,18 +116,18 @@ def tile_transformerblocktpu_pa_kernel(tc, x, rms1_scale, w_qkv, out_0, out_1, o
                     accum_out=mean_sq[b][:],
                 )
 
-        def root(b):
-            nc.scalar.activation(out=rms[b][:], in_=mean_sq[b][:], func=ACT.Sqrt, bias=eps[:])
+        def inverse_rms(b):
+            nc.scalar.activation(
+                out=inv_rms[b][:], in_=mean_sq[b][:], func=ACT.Abs_reciprocal_sqrt, bias=eps[:]
+            )
 
         def normalise(b):
-            inv_rms = per_batch.tile([P, 1], F32, name="inv_rms")
-            nc.vector.reciprocal(out=inv_rms[:], in_=rms[b][:])
             for bank in range(D // N_TILE):
                 feats = slice(bank * N_TILE, (bank + 1) * N_TILE)
                 nc.vector.scalar_tensor_tensor(
                     out=h_sb[b][:, feats],
                     in0=x_sb[b][:, feats],
-                    scalar=inv_rms[:],
+                    scalar=inv_rms[b][:],
                     in1=gain_all[bank][:],
                     op0=ALU.mult,
                     op1=ALU.mult,
@@ -194,7 +194,7 @@ def tile_transformerblocktpu_pa_kernel(tc, x, rms1_scale, w_qkv, out_0, out_1, o
             )
 
         def prepare(u):
-            s = 224 if u == 1 else SCALAR_COLS
+            s = {1: 224, UNITS - 1: 64}.get(u, SCALAR_COLS)
             for c in range(PASSES):
                 regroup(u, c, nc.vector.tensor_copy, 0, N_TILE - s)
                 regroup(u, c, nc.scalar.copy, N_TILE - s, N_TILE)
@@ -224,17 +224,17 @@ def tile_transformerblocktpu_pa_kernel(tc, x, rms1_scale, w_qkv, out_0, out_1, o
                 nc.sync.dma_start(out=outs[j][b, :, cols], in_=result[:])
 
         sum_squares(0)
-        root(0)
+        inverse_rms(0)
         sum_squares(VECTOR_SQUARE)
         normalise(0)
         turned = [turn(0)]
         sum_squares(2)
-        root(1)
-        root(2)
+        inverse_rms(1)
+        inverse_rms(2)
         normalise(1)
         turned.append(turn(1))
         sum_squares(3)
-        root(3)
+        inverse_rms(3)
         normalise(2)
         turned.append(turn(2))
         normalise(3)

@@ -28,6 +28,7 @@ SCALAR_COLS = 112
 UNITS = PROJ * HALVES
 SHARED_UNITS = 1
 VECTOR_SQUARE = 1
+GPSIMD_COLS = 320
 EPS = 1e-6
 
 FLOPS = 2 * BATCH * P * D * PROJ * PROJ_COLS
@@ -239,12 +240,13 @@ def tile_transformerblocktpu_pa_kernel(tc, x, rms1_scale, w_qkv, out_0, out_1, o
         turned.append(turn(2))
         normalise(3)
         turned.append(turn(3))
-        regroup(0, 0, gpsimd_copy, 0, 512)
+        regroup(0, 0, gpsimd_copy, 0, GPSIMD_COLS)
         collect(0, turned[0])
         collect(1, turned[1])
-        regroup(0, 1, nc.scalar.copy, 0, 192)
+        regroup(0, 0, nc.scalar.copy, GPSIMD_COLS, N_TILE)
         collect(2, turned[2])
         collect(3, turned[3])
+        regroup(0, 1, nc.scalar.copy, 0, 192)
         quantise_h(0)
         quantise_h(1)
         regroup(0, 1, nc.vector.tensor_copy, 192, N_TILE)

@@ -24,7 +24,7 @@ PROJ_COLS = 1024
 N_TILE = 512
 HALVES = PROJ_COLS // N_TILE
 RUN = 8
-SCALAR_COLS = 112
+SCALAR_COLS = 80
 UNITS = PROJ * HALVES
 SHARED_UNITS = 1
 VECTOR_SQUARE = 1

@@ -24,7 +24,8 @@ PROJ_COLS = 1024
 N_TILE = 512
 HALVES = PROJ_COLS // N_TILE
 RUN = 8
-SCALAR_COLS = 80
+TENSOR_COLS = 96
+SCALAR_COLS = {1: 128, 2: 32, 3: 32, 4: 32}
 UNITS = PROJ * HALVES
 SHARED_UNITS = 1
 VECTOR_SQUARE = 1
@@ -44,7 +45,7 @@ def tile_transformerblocktpu_pa_kernel(tc, x, rms1_scale, w_qkv, out_0, out_1, o
         keep = ctx.enter_context(tc.tile_pool(name="keep", bufs=1))
         per_batch = ctx.enter_context(tc.tile_pool(name="per_batch", bufs=BATCH))
         w_in = ctx.enter_context(tc.tile_pool(name="w_in", bufs=PROJ * PASSES))
-        w_stage = ctx.enter_context(tc.tile_pool(name="w_stage", bufs=2 * PASSES))
+        w_stage = ctx.enter_context(tc.tile_pool(name="w_stage", bufs=3))
         out_stage = ctx.enter_context(tc.tile_pool(name="out_stage", bufs=3 * BATCH))
         psum = ctx.enter_context(tc.psum_pool(name="psum", bufs=8))
         ctx.enter_context(tc.manual_schedule())
@@ -170,17 +171,32 @@ def tile_transformerblocktpu_pa_kernel(tc, x, rms1_scale, w_qkv, out_0, out_1, o
         w_scales = keep.tile([P, UNITS, PASSES, N_TILE], U8, align_bytes=64)
         w_grouped = {}
 
+        def stage(u):
+            if u not in w_grouped:
+                grouped = w_stage.tile([P, PASSES, N_TILE, PACK], BF16, align_bytes=64, name="grouped")
+                w_grouped[u] = grouped
+            return w_grouped[u]
+
+        def by_run(rows, grouped):
+            return (
+                grouped.rearrange("p (a i) t -> p a t i", i=RUN),
+                rows.rearrange("p t (a i) -> p a t i", i=RUN),
+            )
+
         def regroup(u, c, engine_copy, first, last):
             j, half = divmod(u, HALVES)
-            if (u, c) not in w_grouped:
-                grouped = w_stage.tile([P, N_TILE, PACK], BF16, align_bytes=64, name="grouped")
-                w_grouped[(u, c)] = grouped
             lo = half * N_TILE + first
             hi = half * N_TILE + last
-            engine_copy(
-                w_grouped[(u, c)][:, first:last, :].rearrange("p (a i) t -> p a t i", i=RUN),
-                w_raw[(j, c)][:, :, lo:hi].rearrange("p t (a i) -> p a t i", i=RUN),
-            )
+            engine_copy(*by_run(w_raw[(j, c)][:, :, lo:hi], stage(u)[:, c, first:last, :]))
+
+        def regroup_on_tensor(u):
+            j, half = divmod(u, HALVES)
+            hi = (half + 1) * N_TILE
+            bank = psum.tile([P, PASSES, TENSOR_COLS, PACK], BF16, tag="bank", name="regrouped")
+            for c in range(PASSES):
+                out, rows = by_run(w_raw[(j, c)][:, :, hi - TENSOR_COLS : hi], bank[:, c])
+                nc.tensor.matmul(out=out, lhsT=identity_bf16[:], rhs=rows, start=True, stop=True)
+            nc.scalar.copy(out=stage(u)[:, :, N_TILE - TENSOR_COLS :, :], in_=bank[:])
 
         def gpsimd_copy(out, in_):
             nc.gpsimd.tensor_scalar(
@@ -191,14 +207,16 @@ def tile_transformerblocktpu_pa_kernel(tc, x, rms1_scale, w_qkv, out_0, out_1, o
             nc.vector.quantize_mx(
                 out=w_codes[:, u, c, :].bitcast(FP8X4),
                 scales=w_scales[:, u, c, :],
-                in_=w_grouped[(u, c)][:].rearrange("p n t -> p (n t)"),
+                in_=stage(u)[:, c].rearrange("p n t -> p (n t)"),
             )
 
         def prepare(u):
-            s = {1: 224, UNITS - 1: 64}.get(u, SCALAR_COLS)
+            regroup_on_tensor(u)
+            s = TENSOR_COLS + SCALAR_COLS.get(u, 0)
             for c in range(PASSES):
                 regroup(u, c, nc.vector.tensor_copy, 0, N_TILE - s)
-                regroup(u, c, nc.scalar.copy, N_TILE - s, N_TILE)
+                if u in SCALAR_COLS:
+                    regroup(u, c, nc.scalar.copy, N_TILE - s, N_TILE - TENSOR_COLS)
             for c in range(PASSES):
                 quantise_w(u, c)
 

@@ -24,8 +24,8 @@ PROJ_COLS = 1024
 N_TILE = 512
 HALVES = PROJ_COLS // N_TILE
 RUN = 8
-TENSOR_COLS = 96
-SCALAR_COLS = {1: 128, 2: 32, 3: 32, 4: 32}
+TENSOR_COLS = 112
+SCALAR_COLS = {1: 112, 2: 32, 3: 32, 4: 32}
 UNITS = PROJ * HALVES
 SHARED_UNITS = 1
 VECTOR_SQUARE = 1
@@ -46,7 +46,7 @@ def tile_transformerblocktpu_pa_kernel(tc, x, rms1_scale, w_qkv, out_0, out_1, o
         per_batch = ctx.enter_context(tc.tile_pool(name="per_batch", bufs=BATCH))
         w_in = ctx.enter_context(tc.tile_pool(name="w_in", bufs=PROJ * PASSES))
         w_stage = ctx.enter_context(tc.tile_pool(name="w_stage", bufs=3))
-        out_stage = ctx.enter_context(tc.tile_pool(name="out_stage", bufs=3 * BATCH))
+        out_stage = ctx.enter_context(tc.tile_pool(name="out_stage", bufs=2 * BATCH))
         psum = ctx.enter_context(tc.psum_pool(name="psum", bufs=8))
         ctx.enter_context(tc.manual_schedule())
 
@@ -220,10 +220,13 @@ def tile_transformerblocktpu_pa_kernel(tc, x, rms1_scale, w_qkv, out_0, out_1, o
             for c in range(PASSES):
                 quantise_w(u, c)
 
+        results = {}
+
         def project(u):
             j, half = divmod(u, HALVES)
             cols = slice(half * N_TILE, (half + 1) * N_TILE)
             for b in range(BATCH):
+                wide = j == 0
                 acc = psum.tile([P, N_TILE], F32, tag="bank", name="acc")
                 for c in range(PASSES):
                     nc.tensor.matmul_mx(
@@ -235,12 +238,21 @@ def tile_transformerblocktpu_pa_kernel(tc, x, rms1_scale, w_qkv, out_0, out_1, o
                         start=(c == 0),
                         stop=(c == PASSES - 1),
                     )
-                result = out_stage.tile([P, N_TILE], F32, name="result")
-                if u >= UNITS - SHARED_UNITS and b % 2 == 1:
-                    nc.vector.tensor_copy(out=result[:], in_=acc[:])
+                if not wide:
+                    short = out_stage.tile([P, N_TILE], F32, name="short")
+                    result = short[:]
                 else:
-                    nc.scalar.copy(out=result[:], in_=acc[:])
-                nc.sync.dma_start(out=outs[j][b, :, cols], in_=result[:])
+                    if half == 0:
+                        results[b] = out_stage.tile([P, PROJ_COLS], F32, name="result")
+                    result = results[b][:, cols]
+                if u >= UNITS - SHARED_UNITS and b % 2 == 1:
+                    nc.vector.tensor_copy(out=result, in_=acc[:])
+                else:
+                    nc.scalar.copy(out=result, in_=acc[:])
+                if not wide:
+                    nc.sync.dma_start(out=outs[j][b, :, cols], in_=result)
+                elif half == HALVES - 1:
+                    nc.sync.dma_start(out=outs[j][b], in_=results[b][:])
 
         sum_squares(0)
         inverse_rms(0)

from contextlib import ExitStack

import concourse.masks as masks
import concourse.mybir as mybir

BF16 = mybir.dt.bfloat16
F32 = mybir.dt.float32
U32 = mybir.dt.uint32
U8 = mybir.dt.uint8
I32 = mybir.dt.int32
FP8X4 = mybir.dt.float8_e4m3fn_x4
ACT = mybir.ActivationFunctionType
ALU = mybir.AluOpType

P = 128
PACK = 4
K_PASS = P * PACK
BATCH = 4
D = 1024
PASSES = D // K_PASS
GAIN_ROWS = D // P
PROJ = 3
PROJ_COLS = 1024
N_TILE = 512
HALVES = PROJ_COLS // N_TILE
RUN = 8
TENSOR_COLS = 112
SCALAR_COLS = {1: 112, 2: 32, 3: 32, 4: 32}
UNITS = PROJ * HALVES
SHARED_UNITS = 1
VECTOR_SQUARE = 1
GPSIMD_COLS = 320
EPS = 1e-6

FLOPS = 2 * BATCH * P * D * PROJ * PROJ_COLS


def tile_transformerblocktpu_pa_kernel(tc, x, rms1_scale, w_qkv, out_0, out_1, out_2):
    nc = tc.nc
    outs = [o.rearrange("b s h d -> b s (h d)") for o in (out_0, out_1, out_2)]
    w_rows = w_qkv.rearrange("(c p t) n -> c p t n", t=PACK, p=P)

    with ExitStack() as ctx:
        const = ctx.enter_context(tc.tile_pool(name="const", bufs=1))
        keep = ctx.enter_context(tc.tile_pool(name="keep", bufs=1))
        per_batch = ctx.enter_context(tc.tile_pool(name="per_batch", bufs=BATCH))
        w_in = ctx.enter_context(tc.tile_pool(name="w_in", bufs=PROJ * PASSES))
        w_stage = ctx.enter_context(tc.tile_pool(name="w_stage", bufs=3))
        out_stage = ctx.enter_context(tc.tile_pool(name="out_stage", bufs=2 * BATCH))
        psum = ctx.enter_context(tc.psum_pool(name="psum", bufs=8))
        ctx.enter_context(tc.manual_schedule())

        gain_rows = const.tile([P, P], BF16)
        nc.vector.memset(gain_rows[:].bitcast(I32), 0)
        eps = const.tile([P, 1], F32)
        nc.vector.memset(eps[:], EPS)
        identity_bf16 = const.tile([P, P], BF16)
        masks.make_identity(nc, identity_bf16[:])
        identity = const.tile([P, P], F32)
        masks.make_identity(nc, identity[:])
        warm = const.tile([P, 1], F32)
        nc.scalar.activation(out=warm[:], in_=eps[:], func=ACT.Abs_reciprocal_sqrt)

        x_sb = []
        for b in range(BATCH):
            x_tile = per_batch.tile([P, D], BF16, name="x_tile")
            nc.sync.dma_start(out=x_tile[:], in_=x[b])
            x_sb.append(x_tile)
            if b == 0:
                nc.sync.dma_start(
                    out=gain_rows[0:GAIN_ROWS, :], in_=rms1_scale.rearrange("(r k) -> r k", k=P)
                )
        w_raw = {}
        for j in range(PROJ):
            for c in range(PASSES):
                raw = w_in.tile([P, PACK, PROJ_COLS], BF16, name="w_raw")
                nc.sync.dma_start(
                    out=raw[:], in_=w_rows[c, :, :, j * PROJ_COLS : (j + 1) * PROJ_COLS]
                )
                w_raw[(j, c)] = raw

        gain_all = []
        for bank in range(D // N_TILE):
            spread = psum.tile([P, N_TILE], F32, tag="bank", name="spread")
            for i in range(N_TILE // P):
                r = bank * (N_TILE // P) + i
                nc.tensor.matmul(
                    out=spread[:, i * P : (i + 1) * P],
                    lhsT=identity_bf16[:, r : r + 1].to_broadcast([P, P]),
                    rhs=gain_rows[:],
                    start=True,
                    stop=True,
                )
            gain_all.append(spread)

        mean_sq = [per_batch.tile([P, 1], F32, name="mean_sq") for b in range(BATCH)]
        inv_rms = [per_batch.tile([P, 1], F32, name="inv_rms") for b in range(BATCH)]
        h_sb = [per_batch.tile([P, D], BF16, name="h") for b in range(BATCH)]

        def sum_squares(b):
            squares = per_batch.tile([P, D], BF16, name="squares")
            if b == VECTOR_SQUARE:
                nc.vector.scalar_tensor_tensor(
                    out=squares[:],
                    in0=x_sb[b][:],
                    scalar=1.0 / D,
                    in1=x_sb[b][:],
                    op0=ALU.mult,
                    op1=ALU.mult,
                    accum_out=mean_sq[b][:],
                )
            else:
                nc.scalar.activation(
                    out=squares[:],
                    in_=x_sb[b][:],
                    func=ACT.Square,
                    scale=D**-0.5,
                    accum_out=mean_sq[b][:],
                )

        def inverse_rms(b):
            nc.scalar.activation(
                out=inv_rms[b][:], in_=mean_sq[b][:], func=ACT.Abs_reciprocal_sqrt, bias=eps[:]
            )

        def normalise(b):
            for bank in range(D // N_TILE):
                feats = slice(bank * N_TILE, (bank + 1) * N_TILE)
                nc.vector.scalar_tensor_tensor(
                    out=h_sb[b][:, feats],
                    in0=x_sb[b][:, feats],
                    scalar=inv_rms[b][:],
                    in1=gain_all[bank][:],
                    op0=ALU.mult,
                    op1=ALU.mult,
                )

        h_grouped = keep.tile([P, BATCH, PASSES, P, PACK], BF16, align_bytes=64)
        h_codes = keep.tile([P, BATCH, PASSES * P], U32, align_bytes=64)
        h_scales = keep.tile([P, BATCH, PASSES * P], U8, align_bytes=64)

        def turn(b):
            words = h_sb[b][:].bitcast(F32)
            h_t = psum.tile([P, PASSES, 2, P], F32, tag="bank", name="h_t")
            for c in range(PASSES):
                for u in range(2):
                    w0 = c * (K_PASS // 2)
                    nc.tensor.transpose(
                        out=h_t[:, c, u, :],
                        in_=words[:, w0 + u : w0 + K_PASS // 2 : 2],
                        identity=identity[:],
                    )
            return h_t

        def collect(b, h_t):
            nc.scalar.copy(
                out=h_grouped[:, b].rearrange("p c s t -> p (c s t)").bitcast(F32).rearrange(
                    "p (c s u) -> p c s u", c=PASSES, u=2
                ),
                in_=h_t[:].rearrange("p c u s -> p c s u"),
            )

        def quantise_h(b):
            nc.vector.quantize_mx(
                out=h_codes[:, b, :].bitcast(FP8X4),
                scales=h_scales[:, b, :],
                in_=h_grouped[:, b].rearrange("p c s t -> p (c s t)"),
            )

        w_codes = keep.tile([P, UNITS, PASSES, N_TILE], U32, align_bytes=64)
        w_scales = keep.tile([P, UNITS, PASSES, N_TILE], U8, align_bytes=64)
        w_grouped = {}

        def stage(u):
            if u not in w_grouped:
                grouped = w_stage.tile([P, PASSES, N_TILE, PACK], BF16, align_bytes=64, name="grouped")
                w_grouped[u] = grouped
            return w_grouped[u]

        def by_run(rows, grouped):
            return (
                grouped.rearrange("p (a i) t -> p a t i", i=RUN),
                rows.rearrange("p t (a i) -> p a t i", i=RUN),
            )

        def regroup(u, c, engine_copy, first, last):
            j, half = divmod(u, HALVES)
            lo = half * N_TILE + first
            hi = half * N_TILE + last
            engine_copy(*by_run(w_raw[(j, c)][:, :, lo:hi], stage(u)[:, c, first:last, :]))

        def regroup_on_tensor(u):
            j, half = divmod(u, HALVES)
            hi = (half + 1) * N_TILE
            bank = psum.tile([P, PASSES, TENSOR_COLS, PACK], BF16, tag="bank", name="regrouped")
            for c in range(PASSES):
                out, rows = by_run(w_raw[(j, c)][:, :, hi - TENSOR_COLS : hi], bank[:, c])
                nc.tensor.matmul(out=out, lhsT=identity_bf16[:], rhs=rows, start=True, stop=True)
            nc.scalar.copy(out=stage(u)[:, :, N_TILE - TENSOR_COLS :, :], in_=bank[:])

        def gpsimd_copy(out, in_):
            nc.gpsimd.tensor_scalar(
                out=out, in0=in_, scalar1=1.0, scalar2=0.0, op0=ALU.mult, op1=ALU.add
            )

        def quantise_w(u, c):
            nc.vector.quantize_mx(
                out=w_codes[:, u, c, :].bitcast(FP8X4),
                scales=w_scales[:, u, c, :],
                in_=stage(u)[:, c].rearrange("p n t -> p (n t)"),
            )

        def prepare(u):
            regroup_on_tensor(u)
            s = TENSOR_COLS + SCALAR_COLS.get(u, 0)
            for c in range(PASSES):
                regroup(u, c, nc.vector.tensor_copy, 0, N_TILE - s)
                if u in SCALAR_COLS:
                    regroup(u, c, nc.scalar.copy, N_TILE - s, N_TILE - TENSOR_COLS)
            for c in range(PASSES):
                quantise_w(u, c)

        results = {}

        def project(u):
            j, half = divmod(u, HALVES)
            cols = slice(half * N_TILE, (half + 1) * N_TILE)
            for b in range(BATCH):
                wide = j == 0
                acc = psum.tile([P, N_TILE], F32, tag="bank", name="acc")
                for c in range(PASSES):
                    nc.tensor.matmul_mx(
                        out=acc[:],
                        lhsT=h_codes[:, b, c * P : (c + 1) * P].bitcast(FP8X4),
                        lhsT_scale=h_scales[:, b, c * P : (c + 1) * P],
                        rhs=w_codes[:, u, c, :].bitcast(FP8X4),
                        rhs_scale=w_scales[:, u, c, :],
                        start=(c == 0),
                        stop=(c == PASSES - 1),
                    )
                if not wide:
                    short = out_stage.tile([P, N_TILE], F32, name="short")
                    result = short[:]
                else:
                    if half == 0:
                        results[b] = out_stage.tile([P, PROJ_COLS], F32, name="result")
                    result = results[b][:, cols]
                if u >= UNITS - SHARED_UNITS and b % 2 == 1:
                    nc.vector.tensor_copy(out=result, in_=acc[:])
                else:
                    nc.scalar.copy(out=result, in_=acc[:])
                if not wide:
                    nc.sync.dma_start(out=outs[j][b, :, cols], in_=result)
                elif half == HALVES - 1:
                    nc.sync.dma_start(out=outs[j][b], in_=results[b][:])

        sum_squares(0)
        inverse_rms(0)
        sum_squares(VECTOR_SQUARE)
        normalise(0)
        turned = [turn(0)]
        sum_squares(2)
        inverse_rms(1)
        inverse_rms(2)
        normalise(1)
        turned.append(turn(1))
        sum_squares(3)
        inverse_rms(3)
        normalise(2)
        turned.append(turn(2))
        normalise(3)
        turned.append(turn(3))
        regroup(0, 0, gpsimd_copy, 0, GPSIMD_COLS)
        collect(0, turned[0])
        collect(1, turned[1])
        regroup(0, 0, nc.scalar.copy, GPSIMD_COLS, N_TILE)
        collect(2, turned[2])
        collect(3, turned[3])
        regroup(0, 1, nc.scalar.copy, 0, 192)
        quantise_h(0)
        quantise_h(1)
        regroup(0, 1, nc.vector.tensor_copy, 192, N_TILE)
        quantise_h(2)
        quantise_w(0, 0)
        quantise_h(3)
        quantise_w(0, 1)
        for u in range(UNITS):
            if u + 1 < UNITS:
                prepare(u + 1)
            project(u)
